import numpy as np
import ml_dtypes


def mxq(x, axis, fmt="e4m3"):
    dtype, down = {"e4m3": (ml_dtypes.float8_e4m3fn, 7), "e5m2": (ml_dtypes.float8_e5m2, 14)}[fmt]
    v = np.moveaxis(np.asarray(x, np.float32).astype(ml_dtypes.bfloat16).astype(np.float64), axis, -1)
    blocks = v.reshape(v.shape[:-1] + (-1, 32))
    amax = np.abs(blocks).max(-1, keepdims=True)
    byte = np.maximum(np.where(amax > 0, np.frexp(amax)[1] - 1 + 127, 0) - down, 1)
    scale = np.exp2(byte - 127.0)
    codes = (blocks / scale).astype(np.float32).astype(dtype).astype(np.float64)
    return np.moveaxis((codes * scale).reshape(v.shape), -1, axis)


WIDE = False


def mx_kscale(k):
    if not WIDE:
        return np.ones(k)
    levels = np.array([20, -20, 10, -10, 0])
    a = np.random.permutation(np.resize(levels, k // 512 * 4)).reshape(k // 512, 4)
    idx = np.arange(k)
    return np.exp2(a[idx // 512, idx % 128 // 32])


BF16 = ml_dtypes.bfloat16


def bf(x):
    return np.asarray(x, np.float32).astype(BF16)


def f64(x):
    return np.asarray(x).astype(np.float64)


E, D_NODE, D_EDGE, D_GLOB, LATENT, D_OUT = 8192, 128, 128, 128, 512, 128
D_IN = D_NODE + D_NODE + D_EDGE + D_GLOB
O2 = D_NODE + D_NODE
O3 = O2 + D_EDGE


def concat_input(receiver, sender, edge_attr, global_attr):
    e = edge_attr.shape[0]
    g = np.tile(f64(global_attr), (e // global_attr.shape[0], 1))
    return np.concatenate([f64(receiver), f64(sender), f64(edge_attr), g], axis=1)


def setup_inputs():
    u = mx_kscale(LATENT)
    receiver = bf(np.random.standard_normal((E, D_NODE)))
    sender = bf(np.random.standard_normal((E, D_NODE)))
    edge_attr = bf(np.random.standard_normal((E, D_EDGE)))
    global_attr = bf(np.random.standard_normal((1, D_GLOB)))
    W10 = bf(np.random.standard_normal((D_IN, LATENT)) / np.sqrt(D_IN))
    b1 = bf(np.random.standard_normal(LATENT) * 0.1)
    g = bf(np.random.standard_normal((E, LATENT)) * np.exp2(np.random.randint(-12, 1, (E, 1))) * 16.0 * u)
    z = concat_input(receiver, sender, edge_attr, global_attr) @ f64(W10) + f64(b1)
    return {
        "receiver": receiver,
        "sender": sender,
        "edge_attr": edge_attr,
        "global_attr": global_attr,
        "W1": bf(f64(W10) / u),
        "b1": b1,
        "z": np.asarray(z, np.float32),
        "grad_out": g,
    }


def reference(receiver, sender, edge_attr, global_attr, W1, b1, z, grad_out):
    dz = f64(grad_out) * (f64(z) > 0.0)
    w = f64(W1)[O2:O3]
    return mxq(dz, 1, "e5m2") @ mxq(w, 1, "e4m3").T

@@ -1,0 +1,159 @@
+import concourse.masks as masks
+import concourse.mybir as mybir
+
+F32 = mybir.dt.float32
+BF16 = mybir.dt.bfloat16
+I32 = mybir.dt.int32
+U32 = mybir.dt.uint32
+U8 = mybir.dt.uint8
+E5M2_X4 = mybir.dt.float8_e5m2_x4
+E4M3_X4 = mybir.dt.float8_e4m3fn_x4
+
+P = 128
+EDGES = 8192
+LATENT = 512
+D_EDGE = 128
+W_ROW0 = 256
+
+ROWS = EDGES // P
+WORDS = LATENT // 2
+UNIT_ROWS = 4
+BANK_ROWS = 2
+LOAD_ROWS = 8
+
+FLOPS = 2 * EDGES * LATENT * D_EDGE
+BYTES = EDGES * LATENT * (4 + 2) + D_EDGE * LATENT * 2 + EDGES * D_EDGE * 4
+
+
+def load_sizes():
+    sizes = [LOAD_ROWS] * (ROWS // LOAD_ROWS - 1)
+    rest = LOAD_ROWS
+    while rest > 1:
+        sizes.append(rest // 2)
+        rest -= rest // 2
+    sizes.append(rest)
+    return sizes
+
+
+def tile_edgemodel_pa_v_kernel(
+    tc, receiver, sender, edge_attr, global_attr, W1, b1, z, grad_out, out
+):
+    nc = tc.nc
+
+    z_rows = z.rearrange("(p t) k -> p t k", t=ROWS)
+    g_rows = grad_out.rearrange("(p t) k -> p t k", t=ROWS)
+    out_rows = out.rearrange("(p t) d -> p t d", t=ROWS)
+
+    with (
+        tc.tile_pool(name="const", bufs=1) as const,
+        tc.tile_pool(name="loads", bufs=4) as loads,
+        tc.tile_pool(name="work", bufs=3) as work,
+        tc.psum_pool(name="turned", bufs=4) as turned_pool,
+        tc.psum_pool(name="sums", bufs=3) as sums_pool,
+    ):
+
+        def transpose_words(src_words, n_rows, grouped):
+            grouped_words = grouped.bitcast(F32).rearrange(
+                "q (t c u) -> q t c u", c=P, u=2
+            )
+            for t0 in range(0, n_rows, BANK_ROWS):
+                n = min(BANK_ROWS, n_rows - t0)
+                turned = turned_pool.tile([P, n, 2, P], F32, tag="turned")
+                for t in range(n):
+                    for u in range(2):
+                        first = (t0 + t) * WORDS + u * P
+                        nc.tensor.transpose(
+                            turned[:, t, u, :], src_words[:, first : first + P], identity[:]
+                        )
+                nc.scalar.copy(
+                    out=grouped_words[:, t0 : t0 + n],
+                    in_=turned[:].rearrange("q t u c -> q t c u"),
+                )
+
+        w_sb = const.tile([P, LATENT], BF16)
+        nc.sync.dma_start(out=w_sb[:], in_=W1[W_ROW0 : W_ROW0 + D_EDGE, :])
+        identity = const.tile([P, P], F32)
+        masks.make_identity(nc, identity[:])
+
+        w_codes = const.tile([P, 7 * D_EDGE], U32, align_bytes=64)
+        w_scales = const.tile([P, 7 * D_EDGE], U8, align_bytes=64)
+        nc.vector.memset(w_codes[:].bitcast(I32), 0)
+        nc.vector.memset(w_scales[:].bitcast(I32), 0)
+        w_grouped = const.tile([P, D_EDGE * 4], BF16, align_bytes=64)
+        transpose_words(w_sb[:].bitcast(F32), 1, w_grouped[:])
+        middle = slice(3 * D_EDGE, 4 * D_EDGE)
+        nc.vector.quantize_mx(
+            out=w_codes[:, middle].bitcast(E4M3_X4),
+            scales=w_scales[:, middle],
+            in_=w_grouped[:],
+        )
+
+        def mask_and_transpose(z_sb, g_sb, row0, n_rows):
+            cols = slice(row0 * LATENT, (row0 + n_rows) * LATENT)
+            dz = work.tile([P, n_rows * LATENT], BF16, tag="dz")
+            nc.vector.scalar_tensor_tensor(
+                out=dz[:],
+                in0=z_sb[:, cols],
+                scalar=0.0,
+                in1=g_sb[:, cols],
+                op0=mybir.AluOpType.is_gt,
+                op1=mybir.AluOpType.mult,
+            )
+            grouped = work.tile([P, n_rows * P * 4], BF16, tag="grouped", align_bytes=64)
+            transpose_words(dz[:].bitcast(F32), n_rows, grouped[:])
+            return grouped
+
+        def quantise_and_multiply(grouped, n_rows, out_sb, row0):
+            codes = work.tile([P, n_rows * P], U32, tag="codes", align_bytes=64)
+            scales = work.tile([P, n_rows * P], U8, tag="scales", align_bytes=64)
+            nc.vector.quantize_mx(
+                out=codes[:].bitcast(E5M2_X4), scales=scales[:], in_=grouped[:]
+            )
+            sums = sums_pool.tile([P, UNIT_ROWS * D_EDGE], F32, tag="sums")
+            for j in range(n_rows):
+                edges = slice(j * P, (j + 1) * P)
+                window = slice((3 - j) * D_EDGE, (7 - j) * D_EDGE)
+                nc.tensor.matmul_mx(
+                    out=sums[:],
+                    lhsT=codes[:, edges].bitcast(E5M2_X4),
+                    lhsT_scale=scales[:, edges],
+                    rhs=w_codes[:, window].bitcast(E4M3_X4),
+                    rhs_scale=w_scales[:, window],
+                    start=(j == 0),
+                    stop=(j == n_rows - 1),
+                )
+            nc.scalar.copy(
+                out=out_sb[:, row0 * D_EDGE : (row0 + n_rows) * D_EDGE],
+                in_=sums[:, : n_rows * D_EDGE],
+            )
+
+        def finish(unit):
+            grouped, n_rows, out_sb, row0, first_row, load_rows = unit
+            quantise_and_multiply(grouped, n_rows, out_sb, row0)
+            if row0 + n_rows == load_rows:
+                nc.scalar.dma_start(
+                    out=out_rows[:, first_row : first_row + load_rows, :],
+                    in_=out_sb[:].rearrange("p (t d) -> p t d", d=D_EDGE),
+                )
+
+        waiting = None
+        first_row = 0
+        for load_rows in load_sizes():
+            rows = slice(first_row, first_row + load_rows)
+            g_sb = loads.tile([P, load_rows * LATENT], BF16, tag="g")
+            z_sb = loads.tile([P, load_rows * LATENT], F32, tag="z")
+            nc.sync.dma_start(
+                out=g_sb[:].rearrange("p (t k) -> p t k", k=LATENT), in_=g_rows[:, rows, :]
+            )
+            nc.sync.dma_start(
+                out=z_sb[:].rearrange("p (t k) -> p t k", k=LATENT), in_=z_rows[:, rows, :]
+            )
+            out_sb = work.tile([P, load_rows * D_EDGE], F32, tag="out")
+            for row0 in range(0, load_rows, UNIT_ROWS):
+                n_rows = min(UNIT_ROWS, load_rows - row0)
+                grouped = mask_and_transpose(z_sb, g_sb, row0, n_rows)
+                if waiting is not None:
+                    finish(waiting)
+                waiting = (grouped, n_rows, out_sb, row0, first_row, load_rows)
+            first_row += load_rows
+        finish(waiting)

@@ -20,19 +20,18 @@ WORDS = LATENT // 2
 UNIT_ROWS = 4
 BANK_ROWS = 2
 LOAD_ROWS = 8
+LAG = 2
 
 FLOPS = 2 * EDGES * LATENT * D_EDGE
 BYTES = EDGES * LATENT * (4 + 2) + D_EDGE * LATENT * 2 + EDGES * D_EDGE * 4
 
 
 def load_sizes():
-    sizes = [LOAD_ROWS] * (ROWS // LOAD_ROWS - 1)
-    rest = LOAD_ROWS
-    while rest > 1:
-        sizes.append(rest // 2)
-        rest -= rest // 2
-    sizes.append(rest)
-    return sizes
+    taper = [1]
+    while sum(taper) < LOAD_ROWS:
+        taper.append(sum(taper))
+    full = [LOAD_ROWS] * (ROWS // LOAD_ROWS - 2)
+    return taper + full + list(reversed(taper))
 
 
 def tile_edgemodel_pa_v_kernel(
@@ -47,9 +46,10 @@ def tile_edgemodel_pa_v_kernel(
     with (
         tc.tile_pool(name="const", bufs=1) as const,
         tc.tile_pool(name="loads", bufs=4) as loads,
-        tc.tile_pool(name="work", bufs=3) as work,
+        tc.tile_pool(name="work", bufs=4) as work,
         tc.psum_pool(name="turned", bufs=4) as turned_pool,
         tc.psum_pool(name="sums", bufs=3) as sums_pool,
+        tc.manual_schedule(),
     ):
 
         def transpose_words(src_words, n_rows, grouped):
@@ -103,7 +103,7 @@ def tile_edgemodel_pa_v_kernel(
             transpose_words(dz[:].bitcast(F32), n_rows, grouped[:])
             return grouped
 
-        def quantise_and_multiply(grouped, n_rows, out_sb, row0):
+        def quantise_and_multiply(grouped, n_rows, first_row):
             codes = work.tile([P, n_rows * P], U32, tag="codes", align_bytes=64)
             scales = work.tile([P, n_rows * P], U8, tag="scales", align_bytes=64)
             nc.vector.quantize_mx(
@@ -123,20 +123,14 @@ def tile_edgemodel_pa_v_kernel(
                     stop=(j == n_rows - 1),
                 )
             nc.scalar.copy(
-                out=out_sb[:, row0 * D_EDGE : (row0 + n_rows) * D_EDGE],
+                out=out_sb[:, first_row * D_EDGE : (first_row + n_rows) * D_EDGE],
                 in_=sums[:, : n_rows * D_EDGE],
             )
 
-        def finish(unit):
-            grouped, n_rows, out_sb, row0, first_row, load_rows = unit
-            quantise_and_multiply(grouped, n_rows, out_sb, row0)
-            if row0 + n_rows == load_rows:
-                nc.scalar.dma_start(
-                    out=out_rows[:, first_row : first_row + load_rows, :],
-                    in_=out_sb[:].rearrange("p (t d) -> p t d", d=D_EDGE),
-                )
+        out_sb = const.tile([P, ROWS * D_EDGE], F32)
 
-        waiting = None
+        units = []
+        finished = 0
         first_row = 0
         for load_rows in load_sizes():
             rows = slice(first_row, first_row + load_rows)
@@ -148,12 +142,23 @@ def tile_edgemodel_pa_v_kernel(
             nc.sync.dma_start(
                 out=z_sb[:].rearrange("p (t k) -> p t k", k=LATENT), in_=z_rows[:, rows, :]
             )
-            out_sb = work.tile([P, load_rows * D_EDGE], F32, tag="out")
             for row0 in range(0, load_rows, UNIT_ROWS):
                 n_rows = min(UNIT_ROWS, load_rows - row0)
                 grouped = mask_and_transpose(z_sb, g_sb, row0, n_rows)
-                if waiting is not None:
-                    finish(waiting)
-                waiting = (grouped, n_rows, out_sb, row0, first_row, load_rows)
+                units.append((grouped, n_rows, first_row + row0))
+                if len(units) > finished + LAG:
+                    quantise_and_multiply(*units[finished])
+                    finished += 1
             first_row += load_rows
-        finish(waiting)
+        for unit in units[finished:]:
+            quantise_and_multiply(*unit)
+
+        first_row = 0
+        for load_rows in load_sizes():
+            nc.sync.dma_start(
+                out=out_rows[:, first_row : first_row + load_rows, :],
+                in_=out_sb[:, first_row * D_EDGE : (first_row + load_rows) * D_EDGE].rearrange(
+                    "p (t d) -> p t d", d=D_EDGE
+                ),
+            )
+            first_row += load_rows

@@ -45,7 +45,7 @@ def tile_edgemodel_pa_v_kernel(
 
     with (
         tc.tile_pool(name="const", bufs=1) as const,
-        tc.tile_pool(name="loads", bufs=4) as loads,
+        tc.tile_pool(name="loads", bufs=5) as loads,
         tc.tile_pool(name="work", bufs=4) as work,
         tc.psum_pool(name="turned", bufs=4) as turned_pool,
         tc.psum_pool(name="sums", bufs=3) as sums_pool,

@@ -17,21 +17,28 @@ W_ROW0 = 256
 
 ROWS = EDGES // P
 WORDS = LATENT // 2
-UNIT_ROWS = 4
-BANK_ROWS = 2
+PASS_COLS = 512
+UNIT_ROWS = PASS_COLS // D_EDGE
+BANK_ROWS = PASS_COLS // WORDS
 LOAD_ROWS = 8
-LAG = 2
+LOAD_BUFS = 5
 
 FLOPS = 2 * EDGES * LATENT * D_EDGE
 BYTES = EDGES * LATENT * (4 + 2) + D_EDGE * LATENT * 2 + EDGES * D_EDGE * 4
 
 
+def halves(rows):
+    pieces = []
+    while rows > 1:
+        pieces.append(rows // 2)
+        rows -= rows // 2
+    return pieces + [rows]
+
+
 def load_sizes():
-    taper = [1]
-    while sum(taper) < LOAD_ROWS:
-        taper.append(sum(taper))
-    full = [LOAD_ROWS] * (ROWS // LOAD_ROWS - 2)
-    return taper + full + list(reversed(taper))
+    full = [LOAD_ROWS] * (ROWS // 2 // LOAD_ROWS)
+    half = [LOAD_ROWS // 2] * (ROWS // LOAD_ROWS - 1)
+    return full + half + halves(LOAD_ROWS // 2)
 
 
 def tile_edgemodel_pa_v_kernel(
@@ -45,17 +52,15 @@ def tile_edgemodel_pa_v_kernel(
 
     with (
         tc.tile_pool(name="const", bufs=1) as const,
-        tc.tile_pool(name="loads", bufs=5) as loads,
-        tc.tile_pool(name="work", bufs=4) as work,
+        tc.tile_pool(name="loads", bufs=LOAD_BUFS) as loads,
+        tc.tile_pool(name="work", bufs=3) as work,
         tc.psum_pool(name="turned", bufs=4) as turned_pool,
-        tc.psum_pool(name="sums", bufs=3) as sums_pool,
+        tc.psum_pool(name="sums", bufs=4) as sums_pool,
         tc.manual_schedule(),
     ):
 
         def transpose_words(src_words, n_rows, grouped):
-            grouped_words = grouped.bitcast(F32).rearrange(
-                "q (t c u) -> q t c u", c=P, u=2
-            )
+            grouped_words = grouped.bitcast(F32).rearrange("q (t c u) -> q t c u", c=P, u=2)
             for t0 in range(0, n_rows, BANK_ROWS):
                 n = min(BANK_ROWS, n_rows - t0)
                 turned = turned_pool.tile([P, n, 2, P], F32, tag="turned")
@@ -88,6 +93,8 @@ def tile_edgemodel_pa_v_kernel(
             in_=w_grouped[:],
         )
 
+        out_sb = const.tile([P, ROWS * D_EDGE], F32)
+
         def mask_and_transpose(z_sb, g_sb, row0, n_rows):
             cols = slice(row0 * LATENT, (row0 + n_rows) * LATENT)
             dz = work.tile([P, n_rows * LATENT], BF16, tag="dz")
@@ -109,10 +116,10 @@ def tile_edgemodel_pa_v_kernel(
             nc.vector.quantize_mx(
                 out=codes[:].bitcast(E5M2_X4), scales=scales[:], in_=grouped[:]
             )
-            sums = sums_pool.tile([P, UNIT_ROWS * D_EDGE], F32, tag="sums")
+            sums = sums_pool.tile([P, PASS_COLS], F32, tag="sums")
             for j in range(n_rows):
                 edges = slice(j * P, (j + 1) * P)
-                window = slice((3 - j) * D_EDGE, (7 - j) * D_EDGE)
+                window = slice((3 - j) * D_EDGE, (3 - j) * D_EDGE + PASS_COLS)
                 nc.tensor.matmul_mx(
                     out=sums[:],
                     lhsT=codes[:, edges].bitcast(E5M2_X4),
@@ -127,10 +134,7 @@ def tile_edgemodel_pa_v_kernel(
                 in_=sums[:, : n_rows * D_EDGE],
             )
 
-        out_sb = const.tile([P, ROWS * D_EDGE], F32)
-
-        units = []
-        finished = 0
+        waiting = None
         first_row = 0
         for load_rows in load_sizes():
             rows = slice(first_row, first_row + load_rows)
@@ -145,20 +149,18 @@ def tile_edgemodel_pa_v_kernel(
             for row0 in range(0, load_rows, UNIT_ROWS):
                 n_rows = min(UNIT_ROWS, load_rows - row0)
                 grouped = mask_and_transpose(z_sb, g_sb, row0, n_rows)
-                units.append((grouped, n_rows, first_row + row0))
-                if len(units) > finished + LAG:
-                    quantise_and_multiply(*units[finished])
-                    finished += 1
+                if waiting is not None:
+                    quantise_and_multiply(*waiting)
+                waiting = (grouped, n_rows, first_row + row0)
             first_row += load_rows
-        for unit in units[finished:]:
-            quantise_and_multiply(*unit)
+        quantise_and_multiply(*waiting)
 
         first_row = 0
-        for load_rows in load_sizes():
+        for store_rows in halves(ROWS):
             nc.sync.dma_start(
-                out=out_rows[:, first_row : first_row + load_rows, :],
-                in_=out_sb[:, first_row * D_EDGE : (first_row + load_rows) * D_EDGE].rearrange(
+                out=out_rows[:, first_row : first_row + store_rows, :],
+                in_=out_sb[:, first_row * D_EDGE : (first_row + store_rows) * D_EDGE].rearrange(
                     "p (t d) -> p t d", d=D_EDGE
                 ),
             )
-            first_row += load_rows
+            first_row += store_rows

@@ -20,25 +20,16 @@ WORDS = LATENT // 2
 PASS_COLS = 512
 UNIT_ROWS = PASS_COLS // D_EDGE
 BANK_ROWS = PASS_COLS // WORDS
-LOAD_ROWS = 8
 LOAD_BUFS = 5
+
+LAG = 2
 
 FLOPS = 2 * EDGES * LATENT * D_EDGE
 BYTES = EDGES * LATENT * (4 + 2) + D_EDGE * LATENT * 2 + EDGES * D_EDGE * 4
 
 
-def halves(rows):
-    pieces = []
-    while rows > 1:
-        pieces.append(rows // 2)
-        rows -= rows // 2
-    return pieces + [rows]
-
-
 def load_sizes():
-    full = [LOAD_ROWS] * (ROWS // 2 // LOAD_ROWS)
-    half = [LOAD_ROWS // 2] * (ROWS // LOAD_ROWS - 1)
-    return full + half + halves(LOAD_ROWS // 2)
+    return [8] * 4 + [6] * 4 + [4] * 2
 
 
 def tile_edgemodel_pa_v_kernel(
@@ -53,7 +44,7 @@ def tile_edgemodel_pa_v_kernel(
     with (
         tc.tile_pool(name="const", bufs=1) as const,
         tc.tile_pool(name="loads", bufs=LOAD_BUFS) as loads,
-        tc.tile_pool(name="work", bufs=3) as work,
+        tc.tile_pool(name="work", bufs=LAG + 2) as work,
         tc.psum_pool(name="turned", bufs=4) as turned_pool,
         tc.psum_pool(name="sums", bufs=4) as sums_pool,
         tc.manual_schedule(),
@@ -129,12 +120,25 @@ def tile_edgemodel_pa_v_kernel(
                     start=(j == 0),
                     stop=(j == n_rows - 1),
                 )
+            return sums, n_rows, first_row
+
+        def copy_product(sums, n_rows, first_row):
             nc.scalar.copy(
                 out=out_sb[:, first_row * D_EDGE : (first_row + n_rows) * D_EDGE],
                 in_=sums[:, : n_rows * D_EDGE],
             )
 
-        waiting = None
+        turned_units = []
+        products = []
+
+        def second_half():
+            if products:
+                copy_product(*products[0])
+                products.remove(products[0])
+            if turned_units:
+                products.append(quantise_and_multiply(*turned_units[0]))
+                turned_units.remove(turned_units[0])
+
         first_row = 0
         for load_rows in load_sizes():
             rows = slice(first_row, first_row + load_rows)
@@ -146,17 +150,20 @@ def tile_edgemodel_pa_v_kernel(
             nc.sync.dma_start(
                 out=z_sb[:].rearrange("p (t k) -> p t k", k=LATENT), in_=z_rows[:, rows, :]
             )
-            for row0 in range(0, load_rows, UNIT_ROWS):
-                n_rows = min(UNIT_ROWS, load_rows - row0)
+            row0 = 0
+            while row0 < load_rows:
+                n_rows = min(UNIT_ROWS, load_rows - row0, max(2, (ROWS - first_row - row0) // 2))
                 grouped = mask_and_transpose(z_sb, g_sb, row0, n_rows)
-                if waiting is not None:
-                    quantise_and_multiply(*waiting)
-                waiting = (grouped, n_rows, first_row + row0)
+                turned_units.append((grouped, n_rows, first_row + row0))
+                if len(turned_units) > LAG:
+                    second_half()
+                row0 += n_rows
             first_row += load_rows
-        quantise_and_multiply(*waiting)
+        while turned_units or products:
+            second_half()
 
         first_row = 0
-        for store_rows in halves(ROWS):
+        for store_rows in (32, 16, 8, 4, 2, 2):
             nc.sync.dma_start(
                 out=out_rows[:, first_row : first_row + store_rows, :],
                 in_=out_sb[:, first_row * D_EDGE : (first_row + store_rows) * D_EDGE].rearrange(

@@ -20,7 +20,7 @@ WORDS = LATENT // 2
 PASS_COLS = 512
 UNIT_ROWS = PASS_COLS // D_EDGE
 BANK_ROWS = PASS_COLS // WORDS
-LOAD_BUFS = 5
+LOAD_BUFS = 4
 
 LAG = 2
 
@@ -29,7 +29,7 @@ BYTES = EDGES * LATENT * (4 + 2) + D_EDGE * LATENT * 2 + EDGES * D_EDGE * 4
 
 
 def load_sizes():
-    return [8] * 4 + [6] * 4 + [4] * 2
+    return [12] + [10] * 2 + [8] * 2 + [6] * 2 + [4]
 
 
 def tile_edgemodel_pa_v_kernel(
@@ -86,19 +86,11 @@ def tile_edgemodel_pa_v_kernel(
 
         out_sb = const.tile([P, ROWS * D_EDGE], F32)
 
-        def mask_and_transpose(z_sb, g_sb, row0, n_rows):
+        def mask_and_transpose(mask, g_sb, row0, n_rows):
             cols = slice(row0 * LATENT, (row0 + n_rows) * LATENT)
-            dz = work.tile([P, n_rows * LATENT], BF16, tag="dz")
-            nc.vector.scalar_tensor_tensor(
-                out=dz[:],
-                in0=z_sb[:, cols],
-                scalar=0.0,
-                in1=g_sb[:, cols],
-                op0=mybir.AluOpType.is_gt,
-                op1=mybir.AluOpType.mult,
-            )
+            nc.vector.tensor_mul(g_sb[:, cols], mask[:, cols], g_sb[:, cols])
             grouped = work.tile([P, n_rows * P * 4], BF16, tag="grouped", align_bytes=64)
-            transpose_words(dz[:].bitcast(F32), n_rows, grouped[:])
+            transpose_words(g_sb[:, cols].bitcast(F32), n_rows, grouped[:])
             return grouped
 
         def quantise_and_multiply(grouped, n_rows, first_row):
@@ -131,11 +123,11 @@ def tile_edgemodel_pa_v_kernel(
         turned_units = []
         products = []
 
-        def second_half():
-            if products:
-                copy_product(*products[0])
-                products.remove(products[0])
-            if turned_units:
+        def second_half(lag):
+            for product in products:
+                copy_product(*product)
+            products.clear()
+            if len(turned_units) > lag:
                 products.append(quantise_and_multiply(*turned_units[0]))
                 turned_units.remove(turned_units[0])
 
@@ -145,25 +137,28 @@ def tile_edgemodel_pa_v_kernel(
             g_sb = loads.tile([P, load_rows * LATENT], BF16, tag="g")
             z_sb = loads.tile([P, load_rows * LATENT], F32, tag="z")
             nc.sync.dma_start(
-                out=g_sb[:].rearrange("p (t k) -> p t k", k=LATENT), in_=g_rows[:, rows, :]
+                out=z_sb[:].rearrange("p (t k) -> p t k", k=LATENT), in_=z_rows[:, rows, :]
             )
             nc.sync.dma_start(
-                out=z_sb[:].rearrange("p (t k) -> p t k", k=LATENT), in_=z_rows[:, rows, :]
+                out=g_sb[:].rearrange("p (t k) -> p t k", k=LATENT), in_=g_rows[:, rows, :]
+            )
+            mask = work.tile([P, load_rows * LATENT], BF16, tag="mask", bufs=2)
+            nc.vector.tensor_scalar(
+                out=mask[:], in0=z_sb[:], scalar1=0.0, scalar2=None, op0=mybir.AluOpType.is_gt
             )
             row0 = 0
             while row0 < load_rows:
                 n_rows = min(UNIT_ROWS, load_rows - row0, max(2, (ROWS - first_row - row0) // 2))
-                grouped = mask_and_transpose(z_sb, g_sb, row0, n_rows)
+                grouped = mask_and_transpose(mask, g_sb, row0, n_rows)
                 turned_units.append((grouped, n_rows, first_row + row0))
-                if len(turned_units) > LAG:
-                    second_half()
+                second_half(LAG if first_row + load_rows < ROWS else LAG + 1)
                 row0 += n_rows
             first_row += load_rows
         while turned_units or products:
-            second_half()
+            second_half(0)
 
         first_row = 0
-        for store_rows in (32, 16, 8, 4, 2, 2):
+        for store_rows in (40, 14, 6, 2, 2):
             nc.sync.dma_start(
                 out=out_rows[:, first_row : first_row + store_rows, :],
                 in_=out_sb[:, first_row * D_EDGE : (first_row + store_rows) * D_EDGE].rearrange(

@@ -67,7 +67,7 @@ def tile_edgemodel_pa_v_kernel(
                 )
 
         w_sb = const.tile([P, LATENT], BF16)
-        nc.sync.dma_start(out=w_sb[:], in_=W1[W_ROW0 : W_ROW0 + D_EDGE, :])
+        nc.scalar.dma_start(out=w_sb[:], in_=W1[W_ROW0 : W_ROW0 + D_EDGE, :])
         identity = const.tile([P, P], F32)
         masks.make_identity(nc, identity[:])
 
@@ -158,7 +158,7 @@ def tile_edgemodel_pa_v_kernel(
             second_half(0)
 
         first_row = 0
-        for store_rows in (40, 14, 6, 2, 2):
+        for store_rows in (32, 16, 6, 6, 2, 2):
             nc.sync.dma_start(
                 out=out_rows[:, first_row : first_row + store_rows, :],
                 in_=out_sb[:, first_row * D_EDGE : (first_row + store_rows) * D_EDGE].rearrange(

import concourse.masks as masks
import concourse.mybir as mybir

F32 = mybir.dt.float32
BF16 = mybir.dt.bfloat16
I32 = mybir.dt.int32
U32 = mybir.dt.uint32
U8 = mybir.dt.uint8
E5M2_X4 = mybir.dt.float8_e5m2_x4
E4M3_X4 = mybir.dt.float8_e4m3fn_x4

P = 128
EDGES = 8192
LATENT = 512
D_EDGE = 128
W_ROW0 = 256

ROWS = EDGES // P
WORDS = LATENT // 2
PASS_COLS = 512
UNIT_ROWS = PASS_COLS // D_EDGE
BANK_ROWS = PASS_COLS // WORDS
LOAD_BUFS = 4

LAG = 2

FLOPS = 2 * EDGES * LATENT * D_EDGE
BYTES = EDGES * LATENT * (4 + 2) + D_EDGE * LATENT * 2 + EDGES * D_EDGE * 4


def load_sizes():
    return [12] + [10] * 2 + [8] * 2 + [6] * 2 + [4]


def tile_edgemodel_pa_v_kernel(
    tc, receiver, sender, edge_attr, global_attr, W1, b1, z, grad_out, out
):
    nc = tc.nc

    z_rows = z.rearrange("(p t) k -> p t k", t=ROWS)
    g_rows = grad_out.rearrange("(p t) k -> p t k", t=ROWS)
    out_rows = out.rearrange("(p t) d -> p t d", t=ROWS)

    with (
        tc.tile_pool(name="const", bufs=1) as const,
        tc.tile_pool(name="loads", bufs=LOAD_BUFS) as loads,
        tc.tile_pool(name="work", bufs=LAG + 2) as work,
        tc.psum_pool(name="turned", bufs=4) as turned_pool,
        tc.psum_pool(name="sums", bufs=4) as sums_pool,
        tc.manual_schedule(),
    ):

        def transpose_words(src_words, n_rows, grouped):
            grouped_words = grouped.bitcast(F32).rearrange("q (t c u) -> q t c u", c=P, u=2)
            for t0 in range(0, n_rows, BANK_ROWS):
                n = min(BANK_ROWS, n_rows - t0)
                turned = turned_pool.tile([P, n, 2, P], F32, tag="turned")
                for t in range(n):
                    for u in range(2):
                        first = (t0 + t) * WORDS + u * P
                        nc.tensor.transpose(
                            turned[:, t, u, :], src_words[:, first : first + P], identity[:]
                        )
                nc.scalar.copy(
                    out=grouped_words[:, t0 : t0 + n],
                    in_=turned[:].rearrange("q t u c -> q t c u"),
                )

        w_sb = const.tile([P, LATENT], BF16)
        nc.scalar.dma_start(out=w_sb[:], in_=W1[W_ROW0 : W_ROW0 + D_EDGE, :])
        identity = const.tile([P, P], F32)
        masks.make_identity(nc, identity[:])

        w_codes = const.tile([P, 7 * D_EDGE], U32, align_bytes=64)
        w_scales = const.tile([P, 7 * D_EDGE], U8, align_bytes=64)
        nc.vector.memset(w_codes[:].bitcast(I32), 0)
        nc.vector.memset(w_scales[:].bitcast(I32), 0)
        w_grouped = const.tile([P, D_EDGE * 4], BF16, align_bytes=64)
        transpose_words(w_sb[:].bitcast(F32), 1, w_grouped[:])
        middle = slice(3 * D_EDGE, 4 * D_EDGE)
        nc.vector.quantize_mx(
            out=w_codes[:, middle].bitcast(E4M3_X4),
            scales=w_scales[:, middle],
            in_=w_grouped[:],
        )

        out_sb = const.tile([P, ROWS * D_EDGE], F32)

        def mask_and_transpose(mask, g_sb, row0, n_rows):
            cols = slice(row0 * LATENT, (row0 + n_rows) * LATENT)
            nc.vector.tensor_mul(g_sb[:, cols], mask[:, cols], g_sb[:, cols])
            grouped = work.tile([P, n_rows * P * 4], BF16, tag="grouped", align_bytes=64)
            transpose_words(g_sb[:, cols].bitcast(F32), n_rows, grouped[:])
            return grouped

        def quantise_and_multiply(grouped, n_rows, first_row):
            codes = work.tile([P, n_rows * P], U32, tag="codes", align_bytes=64)
            scales = work.tile([P, n_rows * P], U8, tag="scales", align_bytes=64)
            nc.vector.quantize_mx(
                out=codes[:].bitcast(E5M2_X4), scales=scales[:], in_=grouped[:]
            )
            sums = sums_pool.tile([P, PASS_COLS], F32, tag="sums")
            for j in range(n_rows):
                edges = slice(j * P, (j + 1) * P)
                window = slice((3 - j) * D_EDGE, (3 - j) * D_EDGE + PASS_COLS)
                nc.tensor.matmul_mx(
                    out=sums[:],
                    lhsT=codes[:, edges].bitcast(E5M2_X4),
                    lhsT_scale=scales[:, edges],
                    rhs=w_codes[:, window].bitcast(E4M3_X4),
                    rhs_scale=w_scales[:, window],
                    start=(j == 0),
                    stop=(j == n_rows - 1),
                )
            return sums, n_rows, first_row

        def copy_product(sums, n_rows, first_row):
            nc.scalar.copy(
                out=out_sb[:, first_row * D_EDGE : (first_row + n_rows) * D_EDGE],
                in_=sums[:, : n_rows * D_EDGE],
            )

        turned_units = []
        products = []

        def second_half(lag):
            for product in products:
                copy_product(*product)
            products.clear()
            if len(turned_units) > lag:
                products.append(quantise_and_multiply(*turned_units[0]))
                turned_units.remove(turned_units[0])

        first_row = 0
        for load_rows in load_sizes():
            rows = slice(first_row, first_row + load_rows)
            g_sb = loads.tile([P, load_rows * LATENT], BF16, tag="g")
            z_sb = loads.tile([P, load_rows * LATENT], F32, tag="z")
            nc.sync.dma_start(
                out=z_sb[:].rearrange("p (t k) -> p t k", k=LATENT), in_=z_rows[:, rows, :]
            )
            nc.sync.dma_start(
                out=g_sb[:].rearrange("p (t k) -> p t k", k=LATENT), in_=g_rows[:, rows, :]
            )
            mask = work.tile([P, load_rows * LATENT], BF16, tag="mask", bufs=2)
            nc.vector.tensor_scalar(
                out=mask[:], in0=z_sb[:], scalar1=0.0, scalar2=None, op0=mybir.AluOpType.is_gt
            )
            row0 = 0
            while row0 < load_rows:
                n_rows = min(UNIT_ROWS, load_rows - row0, max(2, (ROWS - first_row - row0) // 2))
                grouped = mask_and_transpose(mask, g_sb, row0, n_rows)
                turned_units.append((grouped, n_rows, first_row + row0))
                second_half(LAG if first_row + load_rows < ROWS else LAG + 1)
                row0 += n_rows
            first_row += load_rows
        while turned_units or products:
            second_half(0)

        first_row = 0
        for store_rows in (32, 16, 6, 6, 2, 2):
            nc.sync.dma_start(
                out=out_rows[:, first_row : first_row + store_rows, :],
                in_=out_sb[:, first_row * D_EDGE : (first_row + store_rows) * D_EDGE].rearrange(
                    "p (t d) -> p t d", d=D_EDGE
                ),
            )
            first_row += store_rows
